import numpy as np
import ml_dtypes


def mxq(x, axis, fmt="e4m3"):
    dtype, down = {"e4m3": (ml_dtypes.float8_e4m3fn, 7), "e5m2": (ml_dtypes.float8_e5m2, 14)}[fmt]
    v = np.moveaxis(np.asarray(x, np.float32).astype(ml_dtypes.bfloat16).astype(np.float64), axis, -1)
    blocks = v.reshape(v.shape[:-1] + (-1, 32))
    amax = np.abs(blocks).max(-1, keepdims=True)
    byte = np.maximum(np.where(amax > 0, np.frexp(amax)[1] - 1 + 127, 0) - down, 1)
    scale = np.exp2(byte - 127.0)
    codes = (blocks / scale).astype(np.float32).astype(dtype).astype(np.float64)
    return np.moveaxis((codes * scale).reshape(v.shape), -1, axis)


WIDE = False


def mx_kscale(k):
    if not WIDE:
        return np.ones(k)
    levels = np.array([10, -10, 5, -5, 0])
    a = np.random.permutation(np.resize(levels, k // 512 * 4)).reshape(k // 512, 4)
    idx = np.arange(k)
    return np.exp2(a[idx // 512, idx % 128 // 32])


BF16 = ml_dtypes.bfloat16


def bf(x):
    return np.asarray(x, np.float32).astype(BF16)


def f64(x):
    return np.asarray(x).astype(np.float64)


STRIDE = 8
MIN_CONFIDENCE = 0.1
B, GH, GW = 8, 32, 64


def setup_inputs():
    Hf, Wf = GH * STRIDE, GW * STRIDE
    A = 2.0 * np.abs(np.log2(mx_kscale(GH * GW))).reshape(GH, GW)
    far = A > 0
    u = np.random.random((B, GH, GW, 2))
    uv = np.random.random((B, GH, GW))
    uc = np.random.random((B, GH, GW))
    variance = f64(bf(np.where(far, 2.0 ** 20 * (1.0 + uv), uv * 60.0 + 4.0)))
    d = np.sqrt(2.0 * variance * (A + 8.0) * np.log(2.0))
    my = np.where(far, np.where(u[..., 1] < 0.5, -d, Hf + d), u[..., 1] * Hf)
    mean = np.stack([u[..., 0] * Wf, my], axis=-1)
    confidence = uc * 2.0 ** A
    return {"mean": bf(mean), "variance": bf(variance), "confidence": bf(confidence)}


def reference(mean, variance, confidence):
    mean, variance, confidence = f64(mean), f64(variance), f64(confidence)
    b, h, w, _ = mean.shape
    Hf, Wf = h * STRIDE, w * STRIDE
    X = np.arange(Wf, dtype=np.float64)
    Y = np.arange(Hf, dtype=np.float64)

    mx = mean[..., 0].reshape(b, -1)
    my = mean[..., 1].reshape(b, -1)
    inv2v = 1.0 / (2.0 * variance.reshape(b, -1))
    conf = confidence.reshape(b, -1)
    conf_m = np.where(conf > MIN_CONFIDENCE, conf, 0.0)

    gy = np.exp(-((Y[None, None, :] - my[:, :, None]) ** 2) * inv2v[:, :, None])
    gx = np.exp(-((X[None, None, :] - mx[:, :, None]) ** 2) * inv2v[:, :, None]) * conf_m[:, :, None]
    acc = mxq(gy, 1, "e4m3").transpose(0, 2, 1) @ mxq(gx, 1, "e4m3")
    return acc

@@ -1,0 +1,251 @@
+from contextlib import ExitStack
+
+import concourse.mybir as mybir
+
+F32 = mybir.dt.float32
+BF16 = mybir.dt.bfloat16
+I32 = mybir.dt.int32
+U32 = mybir.dt.uint32
+U8 = mybir.dt.uint8
+FP8X4 = mybir.dt.float8_e4m3fn_x4
+ACT = mybir.ActivationFunctionType
+ALU = mybir.AluOpType
+
+P = 128
+B = 8
+CELLS = 2048
+HF = 256
+WF = 512
+PACK = 4
+PASSES = CELLS // (P * PACK)
+NQ = B * PASSES * PACK
+MIN_CONFIDENCE = 0.1
+BIG = 1.0e5
+LN2 = 0.6931471805599453
+SQRT2 = 1.4142135623730951
+
+FLOPS = 2 * B * HF * WF * CELLS
+
+DVE_T = (3,)
+
+
+def tile_decodepiflayer_kernel(tc, mean, variance, confidence, out):
+    nc = tc.nc
+    with ExitStack() as ctx:
+        consts = ctx.enter_context(tc.tile_pool(name="consts", bufs=1))
+        upool = ctx.enter_context(tc.tile_pool(name="upool", bufs=2))
+        vpool = ctx.enter_context(tc.tile_pool(name="vpool", bufs=2))
+        sqpool = ctx.enter_context(tc.tile_pool(name="sqpool", bufs=3))
+        dpool = ctx.enter_context(tc.tile_pool(name="dpool", bufs=2))
+        epool = ctx.enter_context(tc.tile_pool(name="epool", bufs=3))
+        gpool = ctx.enter_context(tc.tile_pool(name="gpool", bufs=3))
+        cpool = ctx.enter_context(tc.tile_pool(name="cpool", bufs=3))
+        rpool = ctx.enter_context(tc.tile_pool(name="rpool", bufs=2))
+        psum = ctx.enter_context(tc.psum_pool(name="psum", bufs=2))
+
+        xi = consts.tile([P, WF], I32)
+        nc.gpsimd.iota(xi[:], pattern=[[1, WF]], base=0, channel_multiplier=0)
+        xf = consts.tile([P, WF], F32)
+        nc.vector.tensor_copy(out=xf[:], in_=xi[:])
+
+        vb = consts.tile([P, NQ], BF16)
+        cb = consts.tile([P, NQ], BF16)
+        mb = consts.tile([P, NQ, 2], BF16)
+        var_v = variance.rearrange("b h w -> b (h w)").rearrange(
+            "b (c p t) -> p b c t", c=PASSES, p=P
+        )
+        conf_v = confidence.rearrange("b h w -> b (h w)").rearrange(
+            "b (c p t) -> p b c t", c=PASSES, p=P
+        )
+        mean_v = mean.rearrange("b h w x -> b (h w x)").rearrange(
+            "b (c p k) -> p b c k", c=PASSES, p=P
+        )
+
+        def load(b0, b1, which):
+            q0, q1 = b0 * 16, b1 * 16
+            nb = b1 - b0
+            if which == "v":
+                nc.sync.dma_start(
+                    out=vb[:, q0:q1].rearrange("p (b c t) -> p b c t", b=nb, c=PASSES),
+                    in_=var_v[:, b0:b1],
+                )
+            elif which == "c":
+                nc.sync.dma_start(
+                    out=cb[:, q0:q1].rearrange("p (b c t) -> p b c t", b=nb, c=PASSES),
+                    in_=conf_v[:, b0:b1],
+                )
+            else:
+                nc.sync.dma_start(
+                    out=mb[:, q0:q1, :].rearrange(
+                        "p (b c t) x -> p b c (t x)", b=nb, c=PASSES
+                    ),
+                    in_=mean_v[:, b0:b1],
+                )
+
+        load(0, B, "v")
+        load(0, 1, "m")
+        load(0, 1, "c")
+        load(1, B, "m")
+        load(1, B, "c")
+
+        nm = consts.tile([P, 2, NQ], F32)
+        v2n = consts.tile([P, NQ], F32)
+        ni = consts.tile([P, NQ], F32)
+        s0 = consts.tile([P, NQ], F32)
+        s1 = consts.tile([P, NQ], F32)
+        sv = consts.tile([P, NQ], F32)
+        ta = consts.tile([P, NQ], F32)
+        th = consts.tile([P, NQ], F32)
+        cf = consts.tile([P, NQ], F32)
+        msk = consts.tile([P, NQ], F32)
+        ei = consts.tile([P, NQ], I32)
+        mi = consts.tile([P, NQ], I32)
+        ef = consts.tile([P, NQ], F32)
+        kk = consts.tile([P, NQ], F32)
+        t1 = consts.tile([P, NQ], F32)
+        mp = consts.tile([P, NQ], F32)
+        ek = consts.tile([P, NQ], F32)
+        den = consts.tile([P, NQ], F32)
+        rd = consts.tile([P, NQ], F32)
+        zz = consts.tile([P, NQ], F32)
+        ww = consts.tile([P, NQ], F32)
+        pa = consts.tile([P, NQ], F32)
+        pb = consts.tile([P, NQ], F32)
+        e2 = consts.tile([P, NQ], F32)
+        pen = consts.tile([P, NQ], F32)
+        ll = consts.tile([P, NQ], F32)
+        lb = consts.tile([P, NQ], F32)
+
+        def prep_var(q0, q1):
+            qs = slice(q0, q1)
+            nc.vector.tensor_scalar(
+                out=v2n[:, qs], in0=vb[:, qs], scalar1=-2.0, scalar2=None, op0=ALU.mult
+            )
+            nc.scalar.activation(out=s0[:, qs], in_=v2n[:, qs], func=ACT.Abs_reciprocal_sqrt)
+            nc.vector.reciprocal(out=ni[:, qs], in_=v2n[:, qs])
+            for src, dst in ((s0, s1), (s1, sv)):
+                nc.vector.scalar_tensor_tensor(
+                    out=ta[:, qs], in0=src[:, qs], scalar=0.5, in1=src[:, qs],
+                    op0=ALU.mult, op1=ALU.mult,
+                )
+                nc.vector.tensor_tensor(out=th[:, qs], in0=ta[:, qs], in1=v2n[:, qs], op=ALU.mult)
+                nc.vector.scalar_tensor_tensor(
+                    out=dst[:, qs], in0=th[:, qs], scalar=1.5, in1=src[:, qs],
+                    op0=ALU.add, op1=ALU.mult,
+                )
+
+        def prep_mean(q0, q1):
+            nc.vector.tensor_scalar(
+                out=nm[:, :, q0:q1],
+                in0=mb[:, q0:q1, :].rearrange("p q x -> p x q"),
+                scalar1=-1.0, scalar2=None, op0=ALU.mult,
+            )
+
+        def prep_conf(q0, q1):
+            qs = slice(q0, q1)
+            v = nc.vector
+            v.tensor_copy(out=cf[:, qs], in_=cb[:, qs])
+            v.tensor_scalar(out=msk[:, qs], in0=cf[:, qs], scalar1=MIN_CONFIDENCE, scalar2=None,
+                            op0=ALU.is_gt)
+            v.tensor_scalar(out=ei[:, qs], in0=cf[:, qs].bitcast(I32), scalar1=23, scalar2=None,
+                            op0=ALU.arith_shift_right)
+            v.tensor_scalar(out=mi[:, qs], in0=cf[:, qs].bitcast(I32), scalar1=0x007FFFFF,
+                            scalar2=0x3F800000, op0=ALU.bitwise_and, op1=ALU.bitwise_or)
+            v.tensor_copy(out=ef[:, qs], in_=ei[:, qs])
+            mf = mi[:, qs].bitcast(F32)
+            v.tensor_scalar(out=kk[:, qs], in0=mf, scalar1=SQRT2, scalar2=None, op0=ALU.is_gt)
+            v.tensor_scalar(out=t1[:, qs], in0=kk[:, qs], scalar1=-0.5, scalar2=1.0,
+                            op0=ALU.mult, op1=ALU.add)
+            v.tensor_tensor(out=mp[:, qs], in0=mf, in1=t1[:, qs], op=ALU.mult)
+            v.tensor_tensor(out=ek[:, qs], in0=ef[:, qs], in1=kk[:, qs], op=ALU.add)
+            v.tensor_scalar(out=den[:, qs], in0=mp[:, qs], scalar1=1.0, scalar2=None, op0=ALU.add)
+            v.reciprocal(out=rd[:, qs], in_=den[:, qs])
+            v.scalar_tensor_tensor(out=zz[:, qs], in0=mp[:, qs], scalar=-1.0, in1=rd[:, qs],
+                                   op0=ALU.add, op1=ALU.mult)
+            v.tensor_tensor(out=ww[:, qs], in0=zz[:, qs], in1=zz[:, qs], op=ALU.mult)
+            v.tensor_scalar(out=pa[:, qs], in0=ww[:, qs], scalar1=1.0 / 11.0, scalar2=None,
+                            op0=ALU.mult)
+            cur, nxt = pa, pb
+            for coef in (1.0 / 9.0, 1.0 / 7.0, 1.0 / 5.0, 1.0 / 3.0):
+                v.scalar_tensor_tensor(out=nxt[:, qs], in0=cur[:, qs], scalar=coef, in1=ww[:, qs],
+                                       op0=ALU.add, op1=ALU.mult)
+                cur, nxt = nxt, cur
+            v.scalar_tensor_tensor(out=nxt[:, qs], in0=cur[:, qs], scalar=1.0, in1=zz[:, qs],
+                                   op0=ALU.add, op1=ALU.mult)
+            v.tensor_scalar(out=e2[:, qs], in0=ek[:, qs], scalar1=-127.0, scalar2=LN2,
+                            op0=ALU.add, op1=ALU.mult)
+            v.scalar_tensor_tensor(out=ll[:, qs], in0=nxt[:, qs], scalar=2.0, in1=e2[:, qs],
+                                   op0=ALU.mult, op1=ALU.add)
+            v.tensor_scalar(out=pen[:, qs], in0=msk[:, qs], scalar1=-1.0, scalar2=BIG,
+                            op0=ALU.add, op1=ALU.mult)
+            v.tensor_tensor(out=lb[:, qs], in0=ll[:, qs], in1=pen[:, qs], op=ALU.add)
+
+        prep_var(0, NQ)
+        prep_mean(0, 16)
+        prep_conf(0, 16)
+        prep_mean(16, NQ)
+        prep_conf(16, NQ)
+
+        for b in range(B):
+            acc0 = psum.tile([P, WF], F32)
+            acc1 = psum.tile([P, WF], F32)
+            accs = (acc0, acc1)
+            for c in range(PASSES):
+                q = (b * PASSES + c) * PACK
+                u = upool.tile([P, PACK, HF], F32)
+                for t in range(PACK):
+                    nc.vector.tensor_scalar(
+                        out=u[:, t, :], in0=xf[:, 0:HF],
+                        scalar1=nm[:, 1, q + t : q + t + 1], scalar2=sv[:, q + t : q + t + 1],
+                        op0=ALU.add, op1=ALU.mult,
+                    )
+                v2 = vpool.tile([P, HF, PACK], F32)
+                uperm = u[:].rearrange("p t w -> p w t")
+                nc.vector.tensor_tensor(out=v2[:], in0=uperm, in1=uperm, op=ALU.mult)
+                gy = gpool.tile([P, HF * PACK], BF16, align_bytes=64)
+                nc.scalar.activation(
+                    out=gy[:], in_=v2[:].rearrange("p w t -> p (w t)"), func=ACT.Exp, scale=-1.0
+                )
+                sq = sqpool.tile([P, PACK, WF], F32)
+                for t in range(PACK):
+                    col = nm[:, 0, q + t : q + t + 1]
+                    if t in DVE_T:
+                        d = dpool.tile([P, WF], F32)
+                        nc.vector.tensor_scalar(
+                            out=d[:], in0=xf[:], scalar1=col, scalar2=None, op0=ALU.add
+                        )
+                        nc.vector.tensor_tensor(out=sq[:, t, :], in0=d[:], in1=d[:], op=ALU.mult)
+                    else:
+                        nc.scalar.activation(
+                            out=sq[:, t, :], in_=xf[:], func=ACT.Square, bias=col, scale=1.0
+                        )
+                e = epool.tile([P, PACK, WF], BF16)
+                for t in range(PACK):
+                    nc.scalar.activation(
+                        out=e[:, t, :], in_=sq[:, t, :], func=ACT.Exp,
+                        bias=lb[:, q + t : q + t + 1], scale=ni[:, q + t : q + t + 1],
+                    )
+                gx = gpool.tile([P, WF, PACK], BF16, align_bytes=64)
+                nc.vector.tensor_copy(out=gx[:], in_=e[:].rearrange("p t w -> p w t"))
+
+                gyc = cpool.tile([P, HF], U32, align_bytes=64)
+                gys = cpool.tile([P, HF], U8, align_bytes=64)
+                nc.vector.quantize_mx(out=gyc[:].bitcast(FP8X4), scales=gys[:], in_=gy[:])
+                gxc = cpool.tile([P, WF], U32, align_bytes=64)
+                gxs = cpool.tile([P, WF], U8, align_bytes=64)
+                nc.vector.quantize_mx(
+                    out=gxc[:].bitcast(FP8X4), scales=gxs[:],
+                    in_=gx[:].rearrange("p w t -> p (w t)"),
+                )
+                for m in range(2):
+                    ms = slice(m * P, (m + 1) * P)
+                    nc.tensor.matmul_mx(
+                        out=accs[m][:],
+                        lhsT=gyc[:, ms].bitcast(FP8X4), lhsT_scale=gys[:, ms],
+                        rhs=gxc[:].bitcast(FP8X4), rhs_scale=gxs[:],
+                        start=(c == 0), stop=(c == PASSES - 1),
+                    )
+            res = rpool.tile([P, 2, WF], F32)
+            nc.vector.tensor_copy(out=res[:, 0, :], in_=acc0[:])
+            nc.scalar.copy(out=res[:, 1, :], in_=acc1[:])
+            nc.sync.dma_start(out=out[b].rearrange("(m p) x -> p m x", p=P), in_=res[:])

@@ -27,27 +27,27 @@ SQRT2 = 1.4142135623730951
 FLOPS = 2 * B * HF * WF * CELLS
 
 DVE_T = (3,)
+NU = B * PASSES
 
 
 def tile_decodepiflayer_kernel(tc, mean, variance, confidence, out):
     nc = tc.nc
+    v = nc.vector
     with ExitStack() as ctx:
         consts = ctx.enter_context(tc.tile_pool(name="consts", bufs=1))
         upool = ctx.enter_context(tc.tile_pool(name="upool", bufs=2))
-        vpool = ctx.enter_context(tc.tile_pool(name="vpool", bufs=2))
-        sqpool = ctx.enter_context(tc.tile_pool(name="sqpool", bufs=3))
+        vpool = ctx.enter_context(tc.tile_pool(name="vpool", bufs=3))
+        sqpool = ctx.enter_context(tc.tile_pool(name="sqpool", bufs=4))
         dpool = ctx.enter_context(tc.tile_pool(name="dpool", bufs=2))
         epool = ctx.enter_context(tc.tile_pool(name="epool", bufs=3))
         gpool = ctx.enter_context(tc.tile_pool(name="gpool", bufs=3))
         cpool = ctx.enter_context(tc.tile_pool(name="cpool", bufs=3))
         rpool = ctx.enter_context(tc.tile_pool(name="rpool", bufs=2))
         psum = ctx.enter_context(tc.psum_pool(name="psum", bufs=2))
+        ctx.enter_context(tc.manual_schedule())
 
         xi = consts.tile([P, WF], I32)
-        nc.gpsimd.iota(xi[:], pattern=[[1, WF]], base=0, channel_multiplier=0)
         xf = consts.tile([P, WF], F32)
-        nc.vector.tensor_copy(out=xf[:], in_=xi[:])
-
         vb = consts.tile([P, NQ], BF16)
         cb = consts.tile([P, NQ], BF16)
         mb = consts.tile([P, NQ, 2], BF16)
@@ -61,32 +61,26 @@ def tile_decodepiflayer_kernel(tc, mean, variance, confidence, out):
             "b (c p k) -> p b c k", c=PASSES, p=P
         )
 
-        def load(b0, b1, which):
+        def load(b0, b1):
             q0, q1 = b0 * 16, b1 * 16
             nb = b1 - b0
-            if which == "v":
-                nc.sync.dma_start(
-                    out=vb[:, q0:q1].rearrange("p (b c t) -> p b c t", b=nb, c=PASSES),
-                    in_=var_v[:, b0:b1],
-                )
-            elif which == "c":
-                nc.sync.dma_start(
-                    out=cb[:, q0:q1].rearrange("p (b c t) -> p b c t", b=nb, c=PASSES),
-                    in_=conf_v[:, b0:b1],
-                )
-            else:
-                nc.sync.dma_start(
-                    out=mb[:, q0:q1, :].rearrange(
-                        "p (b c t) x -> p b c (t x)", b=nb, c=PASSES
-                    ),
-                    in_=mean_v[:, b0:b1],
-                )
+            nc.sync.dma_start(
+                out=vb[:, q0:q1].rearrange("p (b c t) -> p b c t", b=nb, c=PASSES),
+                in_=var_v[:, b0:b1],
+            )
+            nc.sync.dma_start(
+                out=mb[:, q0:q1, :].rearrange("p (b c t) x -> p b c (t x)", b=nb, c=PASSES),
+                in_=mean_v[:, b0:b1],
+            )
+            nc.sync.dma_start(
+                out=cb[:, q0:q1].rearrange("p (b c t) -> p b c t", b=nb, c=PASSES),
+                in_=conf_v[:, b0:b1],
+            )
 
-        load(0, B, "v")
-        load(0, 1, "m")
-        load(0, 1, "c")
-        load(1, B, "m")
-        load(1, B, "c")
+        load(0, 1)
+        load(1, B)
+        nc.gpsimd.iota(xi[:], pattern=[[1, WF]], base=0, channel_multiplier=0)
+        v.tensor_copy(out=xf[:], in_=xi[:])
 
         nm = consts.tile([P, 2, NQ], F32)
         v2n = consts.tile([P, NQ], F32)
@@ -116,136 +110,272 @@ def tile_decodepiflayer_kernel(tc, mean, variance, confidence, out):
         ll = consts.tile([P, NQ], F32)
         lb = consts.tile([P, NQ], F32)
 
-        def prep_var(q0, q1):
-            qs = slice(q0, q1)
-            nc.vector.tensor_scalar(
-                out=v2n[:, qs], in0=vb[:, qs], scalar1=-2.0, scalar2=None, op0=ALU.mult
+        def ts(out, in0, s1_, s2_, op0, op1=None):
+            if op1 is None:
+                return lambda: v.tensor_scalar(out=out, in0=in0, scalar1=s1_, scalar2=None, op0=op0)
+            return lambda: v.tensor_scalar(
+                out=out, in0=in0, scalar1=s1_, scalar2=s2_, op0=op0, op1=op1
             )
-            nc.scalar.activation(out=s0[:, qs], in_=v2n[:, qs], func=ACT.Abs_reciprocal_sqrt)
-            nc.vector.reciprocal(out=ni[:, qs], in_=v2n[:, qs])
+
+        def tt(out, in0, in1, op):
+            return lambda: v.tensor_tensor(out=out, in0=in0, in1=in1, op=op)
+
+        def stt(out, in0, scalar, in1, op0, op1):
+            return lambda: v.scalar_tensor_tensor(
+                out=out, in0=in0, scalar=scalar, in1=in1, op0=op0, op1=op1
+            )
+
+        def ops_mean(q0, q1):
+            return [
+                ts(nm[:, :, q0:q1], mb[:, q0:q1, :].rearrange("p q x -> p x q"), -1.0, None, ALU.mult)
+            ]
+
+        def ops_var(q0, q1):
+            qs = slice(q0, q1)
+            return [
+                ts(v2n[:, qs], vb[:, qs], -2.0, None, ALU.mult),
+                lambda: v.reciprocal(out=ni[:, qs], in_=v2n[:, qs]),
+            ]
+
+        def rsqrt(q0, q1):
+            nc.scalar.activation(
+                out=s0[:, q0:q1], in_=vb[:, q0:q1], func=ACT.Abs_reciprocal_sqrt, scale=2.0
+            )
+
+        def ops_newton(q0, q1):
+            qs = slice(q0, q1)
+            ops = []
             for src, dst in ((s0, s1), (s1, sv)):
-                nc.vector.scalar_tensor_tensor(
-                    out=ta[:, qs], in0=src[:, qs], scalar=0.5, in1=src[:, qs],
-                    op0=ALU.mult, op1=ALU.mult,
-                )
-                nc.vector.tensor_tensor(out=th[:, qs], in0=ta[:, qs], in1=v2n[:, qs], op=ALU.mult)
-                nc.vector.scalar_tensor_tensor(
-                    out=dst[:, qs], in0=th[:, qs], scalar=1.5, in1=src[:, qs],
+                ops.append(stt(ta[:, qs], src[:, qs], 0.5, src[:, qs], ALU.mult, ALU.mult))
+                ops.append(tt(th[:, qs], ta[:, qs], v2n[:, qs], ALU.mult))
+                ops.append(stt(dst[:, qs], th[:, qs], 1.5, src[:, qs], ALU.add, ALU.mult))
+            return ops
+
+        def ops_conf(q0, q1):
+            qs = slice(q0, q1)
+            mf = mi[:, qs].bitcast(F32)
+            ops = [
+                lambda: v.tensor_copy(out=cf[:, qs], in_=cb[:, qs]),
+                ts(mi[:, qs], cf[:, qs].bitcast(I32), 0x007FFFFF, 0x3F800000,
+                   ALU.bitwise_and, ALU.bitwise_or),
+                ts(ei[:, qs], cf[:, qs].bitcast(I32), 23, None, ALU.arith_shift_right),
+                ts(kk[:, qs], mf, SQRT2, None, ALU.is_gt),
+                lambda: v.tensor_copy(out=ef[:, qs], in_=ei[:, qs]),
+                ts(t1[:, qs], kk[:, qs], -0.5, 1.0, ALU.mult, ALU.add),
+                tt(ek[:, qs], ef[:, qs], kk[:, qs], ALU.add),
+                tt(mp[:, qs], mf, t1[:, qs], ALU.mult),
+                ts(e2[:, qs], ek[:, qs], -127.0, LN2, ALU.add, ALU.mult),
+                ts(den[:, qs], mp[:, qs], 1.0, None, ALU.add),
+                ts(msk[:, qs], cf[:, qs], MIN_CONFIDENCE, None, ALU.is_gt),
+                lambda: v.reciprocal(out=rd[:, qs], in_=den[:, qs]),
+                ts(pen[:, qs], msk[:, qs], -1.0, BIG, ALU.add, ALU.mult),
+                stt(zz[:, qs], mp[:, qs], -1.0, rd[:, qs], ALU.add, ALU.mult),
+                tt(ww[:, qs], zz[:, qs], zz[:, qs], ALU.mult),
+                ts(pa[:, qs], ww[:, qs], 1.0 / 11.0, None, ALU.mult),
+                stt(pb[:, qs], pa[:, qs], 1.0 / 9.0, ww[:, qs], ALU.add, ALU.mult),
+                stt(pa[:, qs], pb[:, qs], 1.0 / 7.0, ww[:, qs], ALU.add, ALU.mult),
+                stt(pb[:, qs], pa[:, qs], 1.0 / 5.0, ww[:, qs], ALU.add, ALU.mult),
+                stt(pa[:, qs], pb[:, qs], 1.0 / 3.0, ww[:, qs], ALU.add, ALU.mult),
+                stt(pb[:, qs], pa[:, qs], 1.0, zz[:, qs], ALU.add, ALU.mult),
+                stt(ll[:, qs], pb[:, qs], 2.0, e2[:, qs], ALU.mult, ALU.add),
+                tt(lb[:, qs], ll[:, qs], pen[:, qs], ALU.add),
+            ]
+            return ops
+
+        qa = ops_conf(0, 16)
+        qb = ops_var(16, NQ) + ops_newton(16, NQ) + ops_mean(16, NQ) + ops_conf(16, NQ)
+        state = {"a": 0, "b": 0, "b_on": False}
+
+        def pump_a():
+            if state["a"] < len(qa):
+                qa[state["a"]]()
+                state["a"] = state["a"] + 1
+
+        def pump_b():
+            if state["b_on"] and state["b"] < len(qb):
+                qb[state["b"]]()
+                state["b"] = state["b"] + 1
+
+        def pump():
+            pump_a()
+            pump_b()
+
+        for op in ops_mean(0, 16) + ops_var(0, 16):
+            op()
+        rsqrt(0, 16)
+        pump_a()
+        pump_a()
+        for op in ops_newton(0, 16):
+            op()
+            pump_a()
+
+        tiles = {}
+
+        def a_gy_ts(k):
+            if not 0 <= k < NU:
+                return
+            q = k * PACK
+            u = upool.tile([P, PACK, HF], F32)
+            tiles["u", k] = u
+            for t in range(PACK):
+                v.tensor_scalar(
+                    out=u[:, t, :], in0=xf[:, 0:HF],
+                    scalar1=nm[:, 1, q + t : q + t + 1], scalar2=sv[:, q + t : q + t + 1],
                     op0=ALU.add, op1=ALU.mult,
                 )
+                pump()
 
-        def prep_mean(q0, q1):
-            nc.vector.tensor_scalar(
-                out=nm[:, :, q0:q1],
-                in0=mb[:, q0:q1, :].rearrange("p q x -> p x q"),
-                scalar1=-1.0, scalar2=None, op0=ALU.mult,
+        def a_gy_tt(k):
+            if not 0 <= k < NU:
+                return
+            v2 = vpool.tile([P, HF, PACK], F32)
+            tiles["v2", k] = v2
+            uperm = tiles["u", k][:].rearrange("p t w -> p w t")
+            v.tensor_tensor(out=v2[:], in0=uperm, in1=uperm, op=ALU.mult)
+            pump()
+
+        def get_sq(k):
+            if ("sq", k) not in tiles:
+                sq = sqpool.tile([P, PACK, WF], F32)
+                tiles["sq", k] = sq
+            return tiles["sq", k]
+
+        def a_gx_ts(k):
+            if not 0 <= k < NU:
+                return
+            for t in DVE_T:
+                d = dpool.tile([P, WF], F32)
+                tiles["d", k, t] = d
+                v.tensor_scalar(
+                    out=d[:], in0=xf[:], scalar1=nm[:, 0, k * PACK + t : k * PACK + t + 1],
+                    scalar2=None, op0=ALU.add,
+                )
+                pump()
+
+        def a_gx_tt(k):
+            if not 0 <= k < NU:
+                return
+            sq = get_sq(k)
+            for t in DVE_T:
+                d = tiles["d", k, t]
+                v.tensor_tensor(out=sq[:, t, :], in0=d[:], in1=d[:], op=ALU.mult)
+                pump()
+
+        def act_sq(k):
+            if not 0 <= k < NU:
+                return
+            sq = get_sq(k)
+            for t in range(PACK):
+                if t not in DVE_T:
+                    nc.scalar.activation(
+                        out=sq[:, t, :], in_=xf[:], func=ACT.Square,
+                        bias=nm[:, 0, k * PACK + t : k * PACK + t + 1], scale=1.0,
+                    )
+
+        def act_exp_gy(k):
+            if not 0 <= k < NU:
+                return
+            gy = gpool.tile([P, HF * PACK], BF16, align_bytes=64)
+            tiles["gy", k] = gy
+            nc.scalar.activation(
+                out=gy[:], in_=tiles["v2", k][:].rearrange("p w t -> p (w t)"),
+                func=ACT.Exp, scale=-1.0,
             )
 
-        def prep_conf(q0, q1):
-            qs = slice(q0, q1)
-            v = nc.vector
-            v.tensor_copy(out=cf[:, qs], in_=cb[:, qs])
-            v.tensor_scalar(out=msk[:, qs], in0=cf[:, qs], scalar1=MIN_CONFIDENCE, scalar2=None,
-                            op0=ALU.is_gt)
-            v.tensor_scalar(out=ei[:, qs], in0=cf[:, qs].bitcast(I32), scalar1=23, scalar2=None,
-                            op0=ALU.arith_shift_right)
-            v.tensor_scalar(out=mi[:, qs], in0=cf[:, qs].bitcast(I32), scalar1=0x007FFFFF,
-                            scalar2=0x3F800000, op0=ALU.bitwise_and, op1=ALU.bitwise_or)
-            v.tensor_copy(out=ef[:, qs], in_=ei[:, qs])
-            mf = mi[:, qs].bitcast(F32)
-            v.tensor_scalar(out=kk[:, qs], in0=mf, scalar1=SQRT2, scalar2=None, op0=ALU.is_gt)
-            v.tensor_scalar(out=t1[:, qs], in0=kk[:, qs], scalar1=-0.5, scalar2=1.0,
-                            op0=ALU.mult, op1=ALU.add)
-            v.tensor_tensor(out=mp[:, qs], in0=mf, in1=t1[:, qs], op=ALU.mult)
-            v.tensor_tensor(out=ek[:, qs], in0=ef[:, qs], in1=kk[:, qs], op=ALU.add)
-            v.tensor_scalar(out=den[:, qs], in0=mp[:, qs], scalar1=1.0, scalar2=None, op0=ALU.add)
-            v.reciprocal(out=rd[:, qs], in_=den[:, qs])
-            v.scalar_tensor_tensor(out=zz[:, qs], in0=mp[:, qs], scalar=-1.0, in1=rd[:, qs],
-                                   op0=ALU.add, op1=ALU.mult)
-            v.tensor_tensor(out=ww[:, qs], in0=zz[:, qs], in1=zz[:, qs], op=ALU.mult)
-            v.tensor_scalar(out=pa[:, qs], in0=ww[:, qs], scalar1=1.0 / 11.0, scalar2=None,
-                            op0=ALU.mult)
-            cur, nxt = pa, pb
-            for coef in (1.0 / 9.0, 1.0 / 7.0, 1.0 / 5.0, 1.0 / 3.0):
-                v.scalar_tensor_tensor(out=nxt[:, qs], in0=cur[:, qs], scalar=coef, in1=ww[:, qs],
-                                       op0=ALU.add, op1=ALU.mult)
-                cur, nxt = nxt, cur
-            v.scalar_tensor_tensor(out=nxt[:, qs], in0=cur[:, qs], scalar=1.0, in1=zz[:, qs],
-                                   op0=ALU.add, op1=ALU.mult)
-            v.tensor_scalar(out=e2[:, qs], in0=ek[:, qs], scalar1=-127.0, scalar2=LN2,
-                            op0=ALU.add, op1=ALU.mult)
-            v.scalar_tensor_tensor(out=ll[:, qs], in0=nxt[:, qs], scalar=2.0, in1=e2[:, qs],
-                                   op0=ALU.mult, op1=ALU.add)
-            v.tensor_scalar(out=pen[:, qs], in0=msk[:, qs], scalar1=-1.0, scalar2=BIG,
-                            op0=ALU.add, op1=ALU.mult)
-            v.tensor_tensor(out=lb[:, qs], in0=ll[:, qs], in1=pen[:, qs], op=ALU.add)
-
-        prep_var(0, NQ)
-        prep_mean(0, 16)
-        prep_conf(0, 16)
-        prep_mean(16, NQ)
-        prep_conf(16, NQ)
-
-        for b in range(B):
-            acc0 = psum.tile([P, WF], F32)
-            acc1 = psum.tile([P, WF], F32)
-            accs = (acc0, acc1)
-            for c in range(PASSES):
-                q = (b * PASSES + c) * PACK
-                u = upool.tile([P, PACK, HF], F32)
-                for t in range(PACK):
-                    nc.vector.tensor_scalar(
-                        out=u[:, t, :], in0=xf[:, 0:HF],
-                        scalar1=nm[:, 1, q + t : q + t + 1], scalar2=sv[:, q + t : q + t + 1],
-                        op0=ALU.add, op1=ALU.mult,
-                    )
-                v2 = vpool.tile([P, HF, PACK], F32)
-                uperm = u[:].rearrange("p t w -> p w t")
-                nc.vector.tensor_tensor(out=v2[:], in0=uperm, in1=uperm, op=ALU.mult)
-                gy = gpool.tile([P, HF * PACK], BF16, align_bytes=64)
+        def act_exp_gx(k):
+            if not 0 <= k < NU:
+                return
+            q = k * PACK
+            sq = tiles["sq", k]
+            e = epool.tile([P, PACK, WF], BF16)
+            tiles["e", k] = e
+            for t in range(PACK):
                 nc.scalar.activation(
-                    out=gy[:], in_=v2[:].rearrange("p w t -> p (w t)"), func=ACT.Exp, scale=-1.0
+                    out=e[:, t, :], in_=sq[:, t, :], func=ACT.Exp,
+                    bias=lb[:, q + t : q + t + 1], scale=ni[:, q + t : q + t + 1],
                 )
-                sq = sqpool.tile([P, PACK, WF], F32)
-                for t in range(PACK):
-                    col = nm[:, 0, q + t : q + t + 1]
-                    if t in DVE_T:
-                        d = dpool.tile([P, WF], F32)
-                        nc.vector.tensor_scalar(
-                            out=d[:], in0=xf[:], scalar1=col, scalar2=None, op0=ALU.add
-                        )
-                        nc.vector.tensor_tensor(out=sq[:, t, :], in0=d[:], in1=d[:], op=ALU.mult)
-                    else:
-                        nc.scalar.activation(
-                            out=sq[:, t, :], in_=xf[:], func=ACT.Square, bias=col, scale=1.0
-                        )
-                e = epool.tile([P, PACK, WF], BF16)
-                for t in range(PACK):
-                    nc.scalar.activation(
-                        out=e[:, t, :], in_=sq[:, t, :], func=ACT.Exp,
-                        bias=lb[:, q + t : q + t + 1], scale=ni[:, q + t : q + t + 1],
-                    )
-                gx = gpool.tile([P, WF, PACK], BF16, align_bytes=64)
-                nc.vector.tensor_copy(out=gx[:], in_=e[:].rearrange("p t w -> p w t"))
 
-                gyc = cpool.tile([P, HF], U32, align_bytes=64)
-                gys = cpool.tile([P, HF], U8, align_bytes=64)
-                nc.vector.quantize_mx(out=gyc[:].bitcast(FP8X4), scales=gys[:], in_=gy[:])
-                gxc = cpool.tile([P, WF], U32, align_bytes=64)
-                gxs = cpool.tile([P, WF], U8, align_bytes=64)
-                nc.vector.quantize_mx(
-                    out=gxc[:].bitcast(FP8X4), scales=gxs[:],
-                    in_=gx[:].rearrange("p w t -> p (w t)"),
+        def regroup(k):
+            if not 0 <= k < NU:
+                return
+            gx = gpool.tile([P, WF, PACK], BF16, align_bytes=64)
+            tiles["gx", k] = gx
+            v.tensor_copy(out=gx[:], in_=tiles["e", k][:].rearrange("p t w -> p w t"))
+            pump()
+
+        def q_gy(k):
+            if not 0 <= k < NU:
+                return
+            gyc = cpool.tile([P, HF], U32, align_bytes=64)
+            gys = cpool.tile([P, HF], U8, align_bytes=64)
+            tiles["gyc", k] = gyc
+            tiles["gys", k] = gys
+            v.quantize_mx(out=gyc[:].bitcast(FP8X4), scales=gys[:], in_=tiles["gy", k][:])
+            pump()
+
+        def q_gx(k):
+            if not 0 <= k < NU:
+                return
+            gxc = cpool.tile([P, WF], U32, align_bytes=64)
+            gxs = cpool.tile([P, WF], U8, align_bytes=64)
+            tiles["gxc", k] = gxc
+            tiles["gxs", k] = gxs
+            v.quantize_mx(
+                out=gxc[:].bitcast(FP8X4), scales=gxs[:],
+                in_=tiles["gx", k][:].rearrange("p w t -> p (w t)"),
+            )
+            pump()
+
+        def matmuls(k):
+            if not 0 <= k < NU:
+                return
+            b, c = divmod(k, PASSES)
+            if c == 0:
+                acc0 = psum.tile([P, WF], F32)
+                acc1 = psum.tile([P, WF], F32)
+                tiles["acc", b, 0] = acc0
+                tiles["acc", b, 1] = acc1
+            for m in range(2):
+                ms = slice(m * P, (m + 1) * P)
+                nc.tensor.matmul_mx(
+                    out=tiles["acc", b, m][:],
+                    lhsT=tiles["gyc", k][:, ms].bitcast(FP8X4), lhsT_scale=tiles["gys", k][:, ms],
+                    rhs=tiles["gxc", k][:].bitcast(FP8X4), rhs_scale=tiles["gxs", k][:],
+                    start=(c == 0), stop=(c == PASSES - 1),
                 )
-                for m in range(2):
-                    ms = slice(m * P, (m + 1) * P)
-                    nc.tensor.matmul_mx(
-                        out=accs[m][:],
-                        lhsT=gyc[:, ms].bitcast(FP8X4), lhsT_scale=gys[:, ms],
-                        rhs=gxc[:].bitcast(FP8X4), rhs_scale=gxs[:],
-                        start=(c == 0), stop=(c == PASSES - 1),
-                    )
-            res = rpool.tile([P, 2, WF], F32)
-            nc.vector.tensor_copy(out=res[:, 0, :], in_=acc0[:])
-            nc.scalar.copy(out=res[:, 1, :], in_=acc1[:])
-            nc.sync.dma_start(out=out[b].rearrange("(m p) x -> p m x", p=P), in_=res[:])
+
+        def evacuate(k):
+            if not (0 <= k < NU and k % PASSES == PASSES - 1):
+                return
+            b = k // PASSES
+            res0 = rpool.tile([P, WF], F32)
+            res1 = rpool.tile([P, WF], F32)
+            v.tensor_copy(out=res0[:], in_=tiles["acc", b, 0][:])
+            nc.scalar.copy(out=res1[:], in_=tiles["acc", b, 1][:])
+            nc.sync.dma_start(out=out[b, 0:P, :], in_=res0[:])
+            nc.sync.dma_start(out=out[b, P : 2 * P, :], in_=res1[:])
+
+        for i in range(-2, NU + 3):
+            if i == -1:
+                state["b_on"] = True
+            if i == 0:
+                while state["a"] < len(qa):
+                    pump_a()
+            if i == 2:
+                assert state["b"] >= 9
+            if i == 4:
+                assert state["b"] == len(qb)
+            act_sq(i + 2)
+            if i == -1:
+                rsqrt(16, NQ)
+            act_exp_gy(i + 1)
+            act_exp_gx(i)
+            a_gy_ts(i + 2)
+            regroup(i - 1)
+            a_gy_tt(i + 2)
+            a_gx_ts(i + 2)
+            q_gy(i)
+            a_gx_tt(i + 2)
+            q_gx(i - 1)
+            matmuls(i - 1)
+            evacuate(i - 2)

@@ -230,8 +230,10 @@ def tile_decodepiflayer_kernel(tc, mean, variance, confidence, out):
                 return
             v2 = vpool.tile([P, HF, PACK], F32)
             tiles["v2", k] = v2
-            uperm = tiles["u", k][:].rearrange("p t w -> p w t")
-            v.tensor_tensor(out=v2[:], in0=uperm, in1=uperm, op=ALU.mult)
+            uperm = tiles["u", k][:].rearrange("p t (c i) -> p c t i", i=2)
+            v.tensor_tensor(
+                out=v2[:].rearrange("p (c i) t -> p c t i", i=2), in0=uperm, in1=uperm, op=ALU.mult
+            )
             pump()
 
         def get_sq(k):
@@ -300,7 +302,10 @@ def tile_decodepiflayer_kernel(tc, mean, variance, confidence, out):
                 return
             gx = gpool.tile([P, WF, PACK], BF16, align_bytes=64)
             tiles["gx", k] = gx
-            v.tensor_copy(out=gx[:], in_=tiles["e", k][:].rearrange("p t w -> p w t"))
+            v.tensor_copy(
+                out=gx[:].rearrange("p (c i) t -> p c t i", i=4),
+                in_=tiles["e", k][:].rearrange("p t (c i) -> p c t i", i=4),
+            )
             pump()
 
         def q_gy(k):
@@ -368,14 +373,20 @@ def tile_decodepiflayer_kernel(tc, mean, variance, confidence, out):
             act_sq(i + 2)
             if i == -1:
                 rsqrt(16, NQ)
-            act_exp_gy(i + 1)
+            if i + 1 < NU - 1:
+                act_exp_gy(i + 1)
             act_exp_gx(i)
+            if i == NU - 1:
+                act_exp_gy(i)
             a_gy_ts(i + 2)
             regroup(i - 1)
             a_gy_tt(i + 2)
             a_gx_ts(i + 2)
-            q_gy(i)
+            if i < NU - 1:
+                q_gy(i)
             a_gx_tt(i + 2)
             q_gx(i - 1)
+            if i == NU:
+                q_gy(i - 1)
             matmuls(i - 1)
             evacuate(i - 2)

@@ -1,6 +1,7 @@
 from contextlib import ExitStack
 
 import concourse.mybir as mybir
+from concourse.masks import make_identity
 
 F32 = mybir.dt.float32
 BF16 = mybir.dt.bfloat16
@@ -38,12 +39,13 @@ def tile_decodepiflayer_kernel(tc, mean, variance, confidence, out):
         upool = ctx.enter_context(tc.tile_pool(name="upool", bufs=2))
         vpool = ctx.enter_context(tc.tile_pool(name="vpool", bufs=3))
         sqpool = ctx.enter_context(tc.tile_pool(name="sqpool", bufs=4))
-        dpool = ctx.enter_context(tc.tile_pool(name="dpool", bufs=2))
+        dpool = ctx.enter_context(tc.tile_pool(name="dpool", bufs=3))
         epool = ctx.enter_context(tc.tile_pool(name="epool", bufs=3))
         gpool = ctx.enter_context(tc.tile_pool(name="gpool", bufs=3))
         cpool = ctx.enter_context(tc.tile_pool(name="cpool", bufs=3))
         rpool = ctx.enter_context(tc.tile_pool(name="rpool", bufs=2))
         psum = ctx.enter_context(tc.psum_pool(name="psum", bufs=2))
+        xpsum = ctx.enter_context(tc.psum_pool(name="xpsum", bufs=1))
         ctx.enter_context(tc.manual_schedule())
 
         xi = consts.tile([P, WF], I32)
@@ -81,6 +83,10 @@ def tile_decodepiflayer_kernel(tc, mean, variance, confidence, out):
         load(1, B)
         nc.gpsimd.iota(xi[:], pattern=[[1, WF]], base=0, channel_multiplier=0)
         v.tensor_copy(out=xf[:], in_=xi[:])
+        ident = consts.tile([P, P], F32)
+        make_identity(nc, ident[:])
+        xps = xpsum.tile([P, WF], F32)
+        nc.tensor.matmul(out=xps[:], lhsT=ident[:], rhs=xf[:], start=True, stop=True)
 
         nm = consts.tile([P, 2, NQ], F32)
         v2n = consts.tile([P, NQ], F32)
@@ -248,11 +254,10 @@ def tile_decodepiflayer_kernel(tc, mean, variance, confidence, out):
             for t in DVE_T:
                 d = dpool.tile([P, WF], F32)
                 tiles["d", k, t] = d
-                v.tensor_scalar(
+                nc.gpsimd.tensor_scalar(
                     out=d[:], in0=xf[:], scalar1=nm[:, 0, k * PACK + t : k * PACK + t + 1],
-                    scalar2=None, op0=ALU.add,
+                    scalar2=1.0, op0=ALU.add, op1=ALU.mult,
                 )
-                pump()
 
         def a_gx_tt(k):
             if not 0 <= k < NU:
@@ -260,7 +265,10 @@ def tile_decodepiflayer_kernel(tc, mean, variance, confidence, out):
             sq = get_sq(k)
             for t in DVE_T:
                 d = tiles["d", k, t]
-                v.tensor_tensor(out=sq[:, t, :], in0=d[:], in1=d[:], op=ALU.mult)
+                v.scalar_tensor_tensor(
+                    out=sq[:, t, :], in0=xps[:], scalar=nm[:, 0, k * PACK + t : k * PACK + t + 1],
+                    in1=d[:], op0=ALU.add, op1=ALU.mult,
+                )
                 pump()
 
         def act_sq(k):
@@ -356,7 +364,10 @@ def tile_decodepiflayer_kernel(tc, mean, variance, confidence, out):
             res0 = rpool.tile([P, WF], F32)
             res1 = rpool.tile([P, WF], F32)
             v.tensor_copy(out=res0[:], in_=tiles["acc", b, 0][:])
-            nc.scalar.copy(out=res1[:], in_=tiles["acc", b, 1][:])
+            if b == B - 1:
+                nc.scalar.copy(out=res1[:], in_=tiles["acc", b, 1][:])
+            else:
+                v.tensor_copy(out=res1[:], in_=tiles["acc", b, 1][:])
             nc.sync.dma_start(out=out[b, 0:P, :], in_=res0[:])
             nc.sync.dma_start(out=out[b, P : 2 * P, :], in_=res1[:])
 
@@ -366,10 +377,13 @@ def tile_decodepiflayer_kernel(tc, mean, variance, confidence, out):
             if i == 0:
                 while state["a"] < len(qa):
                     pump_a()
-            if i == 2:
+            if i == 1:
                 assert state["b"] >= 9
             if i == 4:
                 assert state["b"] == len(qb)
+            if i == -2:
+                a_gx_ts(0)
+            a_gx_ts(i + 3)
             act_sq(i + 2)
             if i == -1:
                 rsqrt(16, NQ)
@@ -381,7 +395,6 @@ def tile_decodepiflayer_kernel(tc, mean, variance, confidence, out):
             a_gy_ts(i + 2)
             regroup(i - 1)
             a_gy_tt(i + 2)
-            a_gx_ts(i + 2)
             if i < NU - 1:
                 q_gy(i)
             a_gx_tt(i + 2)

@@ -27,8 +27,15 @@ SQRT2 = 1.4142135623730951
 
 FLOPS = 2 * B * HF * WF * CELLS
 
-DVE_T = (3,)
 NU = B * PASSES
+HEAD_UNITS = 5
+TAIL_UNITS = 2
+
+
+def vector_cells(k):
+    if k < HEAD_UNITS or k >= NU - TAIL_UNITS:
+        return ()
+    return (3,)
 
 
 def tile_decodepiflayer_kernel(tc, mean, variance, confidence, out):
@@ -251,7 +258,7 @@ def tile_decodepiflayer_kernel(tc, mean, variance, confidence, out):
         def a_gx_ts(k):
             if not 0 <= k < NU:
                 return
-            for t in DVE_T:
+            for t in vector_cells(k):
                 d = dpool.tile([P, WF], F32)
                 tiles["d", k, t] = d
                 nc.gpsimd.tensor_scalar(
@@ -263,7 +270,7 @@ def tile_decodepiflayer_kernel(tc, mean, variance, confidence, out):
             if not 0 <= k < NU:
                 return
             sq = get_sq(k)
-            for t in DVE_T:
+            for t in vector_cells(k):
                 d = tiles["d", k, t]
                 v.scalar_tensor_tensor(
                     out=sq[:, t, :], in0=xps[:], scalar=nm[:, 0, k * PACK + t : k * PACK + t + 1],
@@ -276,7 +283,7 @@ def tile_decodepiflayer_kernel(tc, mean, variance, confidence, out):
                 return
             sq = get_sq(k)
             for t in range(PACK):
-                if t not in DVE_T:
+                if t not in vector_cells(k):
                     nc.scalar.activation(
                         out=sq[:, t, :], in_=xf[:], func=ACT.Square,
                         bias=nm[:, 0, k * PACK + t : k * PACK + t + 1], scale=1.0,

@@ -13,27 +13,29 @@ ACT = mybir.ActivationFunctionType
 ALU = mybir.AluOpType
 
 P = 128
-B = 8
-CELLS = 2048
-HF = 256
-WF = 512
 PACK = 4
+IMAGES = 8
+CELLS = 2048
+HEIGHT = 256
+WIDTH = 512
 PASSES = CELLS // (P * PACK)
-NQ = B * PASSES * PACK
+UNITS = IMAGES * PASSES
+LAST = UNITS - 1
+COLS = UNITS * PACK
+FIRST = PASSES * PACK
 MIN_CONFIDENCE = 0.1
-BIG = 1.0e5
+MASKED = 1.0e5
 LN2 = 0.6931471805599453
 SQRT2 = 1.4142135623730951
 
-FLOPS = 2 * B * HF * WF * CELLS
-
-NU = B * PASSES
 HEAD_UNITS = 5
 TAIL_UNITS = 2
 
+FLOPS = 2 * IMAGES * HEIGHT * WIDTH * CELLS
+
 
 def vector_cells(k):
-    if k < HEAD_UNITS or k >= NU - TAIL_UNITS:
+    if k < HEAD_UNITS or k >= UNITS - TAIL_UNITS:
         return ()
     return (3,)
 
@@ -55,11 +57,9 @@ def tile_decodepiflayer_kernel(tc, mean, variance, confidence, out):
         xpsum = ctx.enter_context(tc.psum_pool(name="xpsum", bufs=1))
         ctx.enter_context(tc.manual_schedule())
 
-        xi = consts.tile([P, WF], I32)
-        xf = consts.tile([P, WF], F32)
-        vb = consts.tile([P, NQ], BF16)
-        cb = consts.tile([P, NQ], BF16)
-        mb = consts.tile([P, NQ, 2], BF16)
+        vb = consts.tile([P, COLS], BF16)
+        cb = consts.tile([P, COLS], BF16)
+        mb = consts.tile([P, COLS, 2], BF16)
         var_v = variance.rearrange("b h w -> b (h w)").rearrange(
             "b (c p t) -> p b c t", c=PASSES, p=P
         )
@@ -69,344 +69,328 @@ def tile_decodepiflayer_kernel(tc, mean, variance, confidence, out):
         mean_v = mean.rearrange("b h w x -> b (h w x)").rearrange(
             "b (c p k) -> p b c k", c=PASSES, p=P
         )
-
-        def load(b0, b1):
-            q0, q1 = b0 * 16, b1 * 16
-            nb = b1 - b0
+        for b0, b1 in ((0, 1), (1, IMAGES)):
+            cols = slice(b0 * FIRST, b1 * FIRST)
             nc.sync.dma_start(
-                out=vb[:, q0:q1].rearrange("p (b c t) -> p b c t", b=nb, c=PASSES),
+                out=vb[:, cols].rearrange("p (b c t) -> p b c t", b=b1 - b0, c=PASSES),
                 in_=var_v[:, b0:b1],
             )
             nc.sync.dma_start(
-                out=mb[:, q0:q1, :].rearrange("p (b c t) x -> p b c (t x)", b=nb, c=PASSES),
+                out=mb[:, cols, :].rearrange("p (b c t) x -> p b c (t x)", b=b1 - b0, c=PASSES),
                 in_=mean_v[:, b0:b1],
             )
             nc.sync.dma_start(
-                out=cb[:, q0:q1].rearrange("p (b c t) -> p b c t", b=nb, c=PASSES),
+                out=cb[:, cols].rearrange("p (b c t) -> p b c t", b=b1 - b0, c=PASSES),
                 in_=conf_v[:, b0:b1],
             )
 
-        load(0, 1)
-        load(1, B)
-        nc.gpsimd.iota(xi[:], pattern=[[1, WF]], base=0, channel_multiplier=0)
+        xi = consts.tile([P, WIDTH], I32)
+        xf = consts.tile([P, WIDTH], F32)
+        nc.gpsimd.iota(xi[:], pattern=[[1, WIDTH]], base=0, channel_multiplier=0)
         v.tensor_copy(out=xf[:], in_=xi[:])
         ident = consts.tile([P, P], F32)
         make_identity(nc, ident[:])
-        xps = xpsum.tile([P, WF], F32)
+        xps = xpsum.tile([P, WIDTH], F32)
         nc.tensor.matmul(out=xps[:], lhsT=ident[:], rhs=xf[:], start=True, stop=True)
 
-        nm = consts.tile([P, 2, NQ], F32)
-        v2n = consts.tile([P, NQ], F32)
-        ni = consts.tile([P, NQ], F32)
-        s0 = consts.tile([P, NQ], F32)
-        s1 = consts.tile([P, NQ], F32)
-        sv = consts.tile([P, NQ], F32)
-        ta = consts.tile([P, NQ], F32)
-        th = consts.tile([P, NQ], F32)
-        cf = consts.tile([P, NQ], F32)
-        msk = consts.tile([P, NQ], F32)
-        ei = consts.tile([P, NQ], I32)
-        mi = consts.tile([P, NQ], I32)
-        ef = consts.tile([P, NQ], F32)
-        kk = consts.tile([P, NQ], F32)
-        t1 = consts.tile([P, NQ], F32)
-        mp = consts.tile([P, NQ], F32)
-        ek = consts.tile([P, NQ], F32)
-        den = consts.tile([P, NQ], F32)
-        rd = consts.tile([P, NQ], F32)
-        zz = consts.tile([P, NQ], F32)
-        ww = consts.tile([P, NQ], F32)
-        pa = consts.tile([P, NQ], F32)
-        pb = consts.tile([P, NQ], F32)
-        e2 = consts.tile([P, NQ], F32)
-        pen = consts.tile([P, NQ], F32)
-        ll = consts.tile([P, NQ], F32)
-        lb = consts.tile([P, NQ], F32)
+        def column_tile(name, dtype=F32):
+            return consts.tile([P, COLS], dtype, name=name)
 
-        def ts(out, in0, s1_, s2_, op0, op1=None):
+        nm = consts.tile([P, 2, COLS], F32)
+        v2n = column_tile("v2n")
+        ni = column_tile("ni")
+        s0 = column_tile("s0")
+        s1 = column_tile("s1")
+        sv = column_tile("sv")
+        ta = column_tile("ta")
+        th = column_tile("th")
+        cf = column_tile("cf")
+        mi = column_tile("mi", I32)
+        ei = column_tile("ei", I32)
+        ef = column_tile("ef")
+        kk = column_tile("kk")
+        t1 = column_tile("t1")
+        mp = column_tile("mp")
+        ek = column_tile("ek")
+        e2 = column_tile("e2")
+        den = column_tile("den")
+        rd = column_tile("rd")
+        zz = column_tile("zz")
+        ww = column_tile("ww")
+        pa = column_tile("pa")
+        pb = column_tile("pb")
+        msk = column_tile("msk")
+        pen = column_tile("pen")
+        ll = column_tile("ll")
+        lb = column_tile("lb")
+
+        def ts(dst, src, a, b, op0, op1=None):
             if op1 is None:
-                return lambda: v.tensor_scalar(out=out, in0=in0, scalar1=s1_, scalar2=None, op0=op0)
-            return lambda: v.tensor_scalar(
-                out=out, in0=in0, scalar1=s1_, scalar2=s2_, op0=op0, op1=op1
-            )
+                return lambda: v.tensor_scalar(out=dst, in0=src, scalar1=a, scalar2=None, op0=op0)
+            return lambda: v.tensor_scalar(out=dst, in0=src, scalar1=a, scalar2=b, op0=op0, op1=op1)
 
-        def tt(out, in0, in1, op):
-            return lambda: v.tensor_tensor(out=out, in0=in0, in1=in1, op=op)
+        def tt(dst, a, b, op):
+            return lambda: v.tensor_tensor(out=dst, in0=a, in1=b, op=op)
 
-        def stt(out, in0, scalar, in1, op0, op1):
+        def stt(dst, a, scalar, b, op0, op1):
             return lambda: v.scalar_tensor_tensor(
-                out=out, in0=in0, scalar=scalar, in1=in1, op0=op0, op1=op1
+                out=dst, in0=a, scalar=scalar, in1=b, op0=op0, op1=op1
             )
 
-        def ops_mean(q0, q1):
+        def mean_ops(cols):
+            return [ts(nm[:, :, cols], mb[:, cols, :].rearrange("p q x -> p x q"), -1.0, None, ALU.mult)]
+
+        def variance_ops(cols):
             return [
-                ts(nm[:, :, q0:q1], mb[:, q0:q1, :].rearrange("p q x -> p x q"), -1.0, None, ALU.mult)
+                ts(v2n[:, cols], vb[:, cols], -2.0, None, ALU.mult),
+                lambda: v.reciprocal(out=ni[:, cols], in_=v2n[:, cols]),
             ]
 
-        def ops_var(q0, q1):
-            qs = slice(q0, q1)
-            return [
-                ts(v2n[:, qs], vb[:, qs], -2.0, None, ALU.mult),
-                lambda: v.reciprocal(out=ni[:, qs], in_=v2n[:, qs]),
-            ]
-
-        def rsqrt(q0, q1):
+        def rsqrt_on_scalar(cols):
             nc.scalar.activation(
-                out=s0[:, q0:q1], in_=vb[:, q0:q1], func=ACT.Abs_reciprocal_sqrt, scale=2.0
+                out=s0[:, cols], in_=vb[:, cols], func=ACT.Abs_reciprocal_sqrt, scale=2.0
             )
 
-        def ops_newton(q0, q1):
-            qs = slice(q0, q1)
+        def newton_ops(cols):
             ops = []
             for src, dst in ((s0, s1), (s1, sv)):
-                ops.append(stt(ta[:, qs], src[:, qs], 0.5, src[:, qs], ALU.mult, ALU.mult))
-                ops.append(tt(th[:, qs], ta[:, qs], v2n[:, qs], ALU.mult))
-                ops.append(stt(dst[:, qs], th[:, qs], 1.5, src[:, qs], ALU.add, ALU.mult))
+                ops.append(stt(ta[:, cols], src[:, cols], 0.5, src[:, cols], ALU.mult, ALU.mult))
+                ops.append(tt(th[:, cols], ta[:, cols], v2n[:, cols], ALU.mult))
+                ops.append(stt(dst[:, cols], th[:, cols], 1.5, src[:, cols], ALU.add, ALU.mult))
             return ops
 
-        def ops_conf(q0, q1):
-            qs = slice(q0, q1)
-            mf = mi[:, qs].bitcast(F32)
-            ops = [
-                lambda: v.tensor_copy(out=cf[:, qs], in_=cb[:, qs]),
-                ts(mi[:, qs], cf[:, qs].bitcast(I32), 0x007FFFFF, 0x3F800000,
-                   ALU.bitwise_and, ALU.bitwise_or),
-                ts(ei[:, qs], cf[:, qs].bitcast(I32), 23, None, ALU.arith_shift_right),
-                ts(kk[:, qs], mf, SQRT2, None, ALU.is_gt),
-                lambda: v.tensor_copy(out=ef[:, qs], in_=ei[:, qs]),
-                ts(t1[:, qs], kk[:, qs], -0.5, 1.0, ALU.mult, ALU.add),
-                tt(ek[:, qs], ef[:, qs], kk[:, qs], ALU.add),
-                tt(mp[:, qs], mf, t1[:, qs], ALU.mult),
-                ts(e2[:, qs], ek[:, qs], -127.0, LN2, ALU.add, ALU.mult),
-                ts(den[:, qs], mp[:, qs], 1.0, None, ALU.add),
-                ts(msk[:, qs], cf[:, qs], MIN_CONFIDENCE, None, ALU.is_gt),
-                lambda: v.reciprocal(out=rd[:, qs], in_=den[:, qs]),
-                ts(pen[:, qs], msk[:, qs], -1.0, BIG, ALU.add, ALU.mult),
-                stt(zz[:, qs], mp[:, qs], -1.0, rd[:, qs], ALU.add, ALU.mult),
-                tt(ww[:, qs], zz[:, qs], zz[:, qs], ALU.mult),
-                ts(pa[:, qs], ww[:, qs], 1.0 / 11.0, None, ALU.mult),
-                stt(pb[:, qs], pa[:, qs], 1.0 / 9.0, ww[:, qs], ALU.add, ALU.mult),
-                stt(pa[:, qs], pb[:, qs], 1.0 / 7.0, ww[:, qs], ALU.add, ALU.mult),
-                stt(pb[:, qs], pa[:, qs], 1.0 / 5.0, ww[:, qs], ALU.add, ALU.mult),
-                stt(pa[:, qs], pb[:, qs], 1.0 / 3.0, ww[:, qs], ALU.add, ALU.mult),
-                stt(pb[:, qs], pa[:, qs], 1.0, zz[:, qs], ALU.add, ALU.mult),
-                stt(ll[:, qs], pb[:, qs], 2.0, e2[:, qs], ALU.mult, ALU.add),
-                tt(lb[:, qs], ll[:, qs], pen[:, qs], ALU.add),
+        def confidence_ops(cols):
+            bits = cf[:, cols].bitcast(I32)
+            m = mi[:, cols].bitcast(F32)
+            return [
+                lambda: v.tensor_copy(out=cf[:, cols], in_=cb[:, cols]),
+                ts(mi[:, cols], bits, 0x007FFFFF, 0x3F800000, ALU.bitwise_and, ALU.bitwise_or),
+                ts(ei[:, cols], bits, 23, None, ALU.arith_shift_right),
+                ts(kk[:, cols], m, SQRT2, None, ALU.is_gt),
+                lambda: v.tensor_copy(out=ef[:, cols], in_=ei[:, cols]),
+                ts(t1[:, cols], kk[:, cols], -0.5, 1.0, ALU.mult, ALU.add),
+                tt(ek[:, cols], ef[:, cols], kk[:, cols], ALU.add),
+                tt(mp[:, cols], m, t1[:, cols], ALU.mult),
+                ts(e2[:, cols], ek[:, cols], -127.0, LN2, ALU.add, ALU.mult),
+                ts(den[:, cols], mp[:, cols], 1.0, None, ALU.add),
+                ts(msk[:, cols], cf[:, cols], MIN_CONFIDENCE, None, ALU.is_gt),
+                lambda: v.reciprocal(out=rd[:, cols], in_=den[:, cols]),
+                ts(pen[:, cols], msk[:, cols], -1.0, MASKED, ALU.add, ALU.mult),
+                stt(zz[:, cols], mp[:, cols], -1.0, rd[:, cols], ALU.add, ALU.mult),
+                tt(ww[:, cols], zz[:, cols], zz[:, cols], ALU.mult),
+                ts(pa[:, cols], ww[:, cols], 1.0 / 11.0, None, ALU.mult),
+                stt(pb[:, cols], pa[:, cols], 1.0 / 9.0, ww[:, cols], ALU.add, ALU.mult),
+                stt(pa[:, cols], pb[:, cols], 1.0 / 7.0, ww[:, cols], ALU.add, ALU.mult),
+                stt(pb[:, cols], pa[:, cols], 1.0 / 5.0, ww[:, cols], ALU.add, ALU.mult),
+                stt(pa[:, cols], pb[:, cols], 1.0 / 3.0, ww[:, cols], ALU.add, ALU.mult),
+                stt(pb[:, cols], pa[:, cols], 1.0, zz[:, cols], ALU.add, ALU.mult),
+                stt(ll[:, cols], pb[:, cols], 2.0, e2[:, cols], ALU.mult, ALU.add),
+                tt(lb[:, cols], ll[:, cols], pen[:, cols], ALU.add),
             ]
-            return ops
 
-        qa = ops_conf(0, 16)
-        qb = ops_var(16, NQ) + ops_newton(16, NQ) + ops_mean(16, NQ) + ops_conf(16, NQ)
-        state = {"a": 0, "b": 0, "b_on": False}
+        first = slice(0, FIRST)
+        rest = slice(FIRST, COLS)
+        queues = {"first": confidence_ops(first), "rest": []}
+        issued = {"first": 0, "rest": 0}
 
-        def pump_a():
-            if state["a"] < len(qa):
-                qa[state["a"]]()
-                state["a"] = state["a"] + 1
+        def issue(name):
+            if issued[name] < len(queues[name]):
+                queues[name][issued[name]]()
+                issued[name] = issued[name] + 1
 
-        def pump_b():
-            if state["b_on"] and state["b"] < len(qb):
-                qb[state["b"]]()
-                state["b"] = state["b"] + 1
+        def fill():
+            issue("first")
+            issue("rest")
 
-        def pump():
-            pump_a()
-            pump_b()
-
-        for op in ops_mean(0, 16) + ops_var(0, 16):
+        for op in mean_ops(first) + variance_ops(first):
             op()
-        rsqrt(0, 16)
-        pump_a()
-        pump_a()
-        for op in ops_newton(0, 16):
+        rsqrt_on_scalar(first)
+        issue("first")
+        issue("first")
+        for op in newton_ops(first):
             op()
-            pump_a()
+            issue("first")
 
         tiles = {}
 
-        def a_gy_ts(k):
-            if not 0 <= k < NU:
-                return
-            q = k * PACK
-            u = upool.tile([P, PACK, HF], F32)
+        def col(tile, k, t):
+            return tile[:, k * PACK + t : k * PACK + t + 1]
+
+        def scaled_dy(k):
+            u = upool.tile([P, PACK, HEIGHT], F32)
             tiles["u", k] = u
             for t in range(PACK):
                 v.tensor_scalar(
-                    out=u[:, t, :], in0=xf[:, 0:HF],
-                    scalar1=nm[:, 1, q + t : q + t + 1], scalar2=sv[:, q + t : q + t + 1],
-                    op0=ALU.add, op1=ALU.mult,
+                    out=u[:, t, :], in0=xf[:, 0:HEIGHT], scalar1=col(nm[:, 1, :], k, t),
+                    scalar2=col(sv, k, t), op0=ALU.add, op1=ALU.mult,
                 )
-                pump()
+                fill()
 
-        def a_gy_tt(k):
-            if not 0 <= k < NU:
-                return
-            v2 = vpool.tile([P, HF, PACK], F32)
+        def square_dy(k):
+            v2 = vpool.tile([P, HEIGHT, PACK], F32)
             tiles["v2", k] = v2
-            uperm = tiles["u", k][:].rearrange("p t (c i) -> p c t i", i=2)
+            pairs = tiles["u", k][:].rearrange("p t (c i) -> p c t i", i=2)
             v.tensor_tensor(
-                out=v2[:].rearrange("p (c i) t -> p c t i", i=2), in0=uperm, in1=uperm, op=ALU.mult
+                out=v2[:].rearrange("p (c i) t -> p c t i", i=2), in0=pairs, in1=pairs, op=ALU.mult
             )
-            pump()
+            fill()
 
-        def get_sq(k):
+        def exp_gy(k):
+            pieces = 2 if k == LAST else 1
+            gy = gpool.tile([P, HEIGHT * PACK], BF16, align_bytes=64)
+            tiles["gy", k] = gy
+            flat = tiles["v2", k][:].rearrange("p w t -> p (w t)")
+            width = HEIGHT * PACK // pieces
+            for h in range(pieces):
+                part = slice(h * width, (h + 1) * width)
+                nc.scalar.activation(out=gy[:, part], in_=flat[:, part], func=ACT.Exp, scale=-1.0)
+
+        def quantise_gy(k):
+            pieces = 2 if k == LAST else 1
+            gyc = cpool.tile([P, HEIGHT], U32, align_bytes=64)
+            gys = cpool.tile([P, HEIGHT], U8, align_bytes=64)
+            tiles["gyc", k] = gyc
+            tiles["gys", k] = gys
+            width = HEIGHT // pieces
+            for h in range(pieces):
+                part = slice(h * width, (h + 1) * width)
+                v.quantize_mx(
+                    out=gyc[:, part].bitcast(FP8X4), scales=gys[:, part],
+                    in_=tiles["gy", k][:, h * width * PACK : (h + 1) * width * PACK],
+                )
+                fill()
+
+        def squares_tile(k):
             if ("sq", k) not in tiles:
-                sq = sqpool.tile([P, PACK, WF], F32)
+                sq = sqpool.tile([P, PACK, WIDTH], F32)
                 tiles["sq", k] = sq
             return tiles["sq", k]
 
-        def a_gx_ts(k):
-            if not 0 <= k < NU:
-                return
+        def dx_on_gpsimd(k):
             for t in vector_cells(k):
-                d = dpool.tile([P, WF], F32)
+                d = dpool.tile([P, WIDTH], F32)
                 tiles["d", k, t] = d
                 nc.gpsimd.tensor_scalar(
-                    out=d[:], in0=xf[:], scalar1=nm[:, 0, k * PACK + t : k * PACK + t + 1],
-                    scalar2=1.0, op0=ALU.add, op1=ALU.mult,
+                    out=d[:], in0=xf[:], scalar1=col(nm[:, 0, :], k, t), scalar2=1.0,
+                    op0=ALU.add, op1=ALU.mult,
                 )
 
-        def a_gx_tt(k):
-            if not 0 <= k < NU:
-                return
-            sq = get_sq(k)
+        def squares_on_vector(k):
+            sq = squares_tile(k)
             for t in vector_cells(k):
-                d = tiles["d", k, t]
                 v.scalar_tensor_tensor(
-                    out=sq[:, t, :], in0=xps[:], scalar=nm[:, 0, k * PACK + t : k * PACK + t + 1],
-                    in1=d[:], op0=ALU.add, op1=ALU.mult,
+                    out=sq[:, t, :], in0=xps[:], scalar=col(nm[:, 0, :], k, t),
+                    in1=tiles["d", k, t][:], op0=ALU.add, op1=ALU.mult,
                 )
-                pump()
+                fill()
 
-        def act_sq(k):
-            if not 0 <= k < NU:
-                return
-            sq = get_sq(k)
+        def squares_on_scalar(k):
+            sq = squares_tile(k)
             for t in range(PACK):
                 if t not in vector_cells(k):
                     nc.scalar.activation(
                         out=sq[:, t, :], in_=xf[:], func=ACT.Square,
-                        bias=nm[:, 0, k * PACK + t : k * PACK + t + 1], scale=1.0,
+                        bias=mb[:, k * PACK + t, 0:1], scale=-1.0,
                     )
 
-        def act_exp_gy(k):
-            if not 0 <= k < NU:
-                return
-            gy = gpool.tile([P, HF * PACK], BF16, align_bytes=64)
-            tiles["gy", k] = gy
-            nc.scalar.activation(
-                out=gy[:], in_=tiles["v2", k][:].rearrange("p w t -> p (w t)"),
-                func=ACT.Exp, scale=-1.0,
-            )
-
-        def act_exp_gx(k):
-            if not 0 <= k < NU:
-                return
-            q = k * PACK
-            sq = tiles["sq", k]
-            e = epool.tile([P, PACK, WF], BF16)
+        def exp_gx(k):
+            e = epool.tile([P, PACK, WIDTH], BF16)
             tiles["e", k] = e
             for t in range(PACK):
                 nc.scalar.activation(
-                    out=e[:, t, :], in_=sq[:, t, :], func=ACT.Exp,
-                    bias=lb[:, q + t : q + t + 1], scale=ni[:, q + t : q + t + 1],
+                    out=e[:, t, :], in_=tiles["sq", k][:, t, :], func=ACT.Exp,
+                    bias=col(lb, k, t), scale=col(ni, k, t),
                 )
 
-        def regroup(k):
-            if not 0 <= k < NU:
-                return
-            gx = gpool.tile([P, WF, PACK], BF16, align_bytes=64)
+        def regroup_gx(k):
+            gx = gpool.tile([P, WIDTH, PACK], BF16, align_bytes=64)
             tiles["gx", k] = gx
             v.tensor_copy(
                 out=gx[:].rearrange("p (c i) t -> p c t i", i=4),
                 in_=tiles["e", k][:].rearrange("p t (c i) -> p c t i", i=4),
             )
-            pump()
+            fill()
 
-        def q_gy(k):
-            if not 0 <= k < NU:
-                return
-            gyc = cpool.tile([P, HF], U32, align_bytes=64)
-            gys = cpool.tile([P, HF], U8, align_bytes=64)
-            tiles["gyc", k] = gyc
-            tiles["gys", k] = gys
-            v.quantize_mx(out=gyc[:].bitcast(FP8X4), scales=gys[:], in_=tiles["gy", k][:])
-            pump()
-
-        def q_gx(k):
-            if not 0 <= k < NU:
-                return
-            gxc = cpool.tile([P, WF], U32, align_bytes=64)
-            gxs = cpool.tile([P, WF], U8, align_bytes=64)
+        def quantise_gx(k):
+            gxc = cpool.tile([P, WIDTH], U32, align_bytes=64)
+            gxs = cpool.tile([P, WIDTH], U8, align_bytes=64)
             tiles["gxc", k] = gxc
             tiles["gxs", k] = gxs
             v.quantize_mx(
                 out=gxc[:].bitcast(FP8X4), scales=gxs[:],
                 in_=tiles["gx", k][:].rearrange("p w t -> p (w t)"),
             )
-            pump()
+            fill()
 
         def matmuls(k):
-            if not 0 <= k < NU:
-                return
             b, c = divmod(k, PASSES)
             if c == 0:
-                acc0 = psum.tile([P, WF], F32)
-                acc1 = psum.tile([P, WF], F32)
+                acc0 = psum.tile([P, WIDTH], F32)
+                acc1 = psum.tile([P, WIDTH], F32)
                 tiles["acc", b, 0] = acc0
                 tiles["acc", b, 1] = acc1
-            for m in range(2):
-                ms = slice(m * P, (m + 1) * P)
+            for m in range(HEIGHT // P):
+                rows = slice(m * P, (m + 1) * P)
                 nc.tensor.matmul_mx(
                     out=tiles["acc", b, m][:],
-                    lhsT=tiles["gyc", k][:, ms].bitcast(FP8X4), lhsT_scale=tiles["gys", k][:, ms],
-                    rhs=tiles["gxc", k][:].bitcast(FP8X4), rhs_scale=tiles["gxs", k][:],
-                    start=(c == 0), stop=(c == PASSES - 1),
+                    lhsT=tiles["gyc", k][:, rows].bitcast(FP8X4),
+                    lhsT_scale=tiles["gys", k][:, rows],
+                    rhs=tiles["gxc", k][:].bitcast(FP8X4),
+                    rhs_scale=tiles["gxs", k][:],
+                    start=(c == 0),
+                    stop=(c == PASSES - 1),
                 )
 
-        def evacuate(k):
-            if not (0 <= k < NU and k % PASSES == PASSES - 1):
+        def store(k):
+            b, c = divmod(k, PASSES)
+            if c != PASSES - 1:
                 return
-            b = k // PASSES
-            res0 = rpool.tile([P, WF], F32)
-            res1 = rpool.tile([P, WF], F32)
+            res0 = rpool.tile([P, WIDTH], F32)
+            res1 = rpool.tile([P, WIDTH], F32)
             v.tensor_copy(out=res0[:], in_=tiles["acc", b, 0][:])
-            if b == B - 1:
+            if k == LAST:
                 nc.scalar.copy(out=res1[:], in_=tiles["acc", b, 1][:])
             else:
                 v.tensor_copy(out=res1[:], in_=tiles["acc", b, 1][:])
             nc.sync.dma_start(out=out[b, 0:P, :], in_=res0[:])
             nc.sync.dma_start(out=out[b, P : 2 * P, :], in_=res1[:])
 
-        for i in range(-2, NU + 3):
+        def stage(fn, k):
+            if 0 <= k < UNITS:
+                fn(k)
+
+        needed_first = variance_ops(rest) + newton_ops(rest) + mean_ops(rest)
+        stage(dx_on_gpsimd, 0)
+        for i in range(-2, UNITS + 2):
             if i == -1:
-                state["b_on"] = True
+                queues["rest"].extend(needed_first + confidence_ops(rest))
             if i == 0:
-                while state["a"] < len(qa):
-                    pump_a()
-            if i == 1:
-                assert state["b"] >= 9
-            if i == 4:
-                assert state["b"] == len(qb)
-            if i == -2:
-                a_gx_ts(0)
-            a_gx_ts(i + 3)
-            act_sq(i + 2)
+                while issued["first"] < len(queues["first"]):
+                    issue("first")
+            if i == PASSES - 2:
+                assert issued["rest"] >= len(needed_first)
+            if i == PASSES:
+                assert issued["rest"] == len(queues["rest"])
+
+            stage(dx_on_gpsimd, i + 3)
+
+            stage(squares_on_scalar, i + 2)
             if i == -1:
-                rsqrt(16, NQ)
-            if i + 1 < NU - 1:
-                act_exp_gy(i + 1)
-            act_exp_gx(i)
-            if i == NU - 1:
-                act_exp_gy(i)
-            a_gy_ts(i + 2)
-            regroup(i - 1)
-            a_gy_tt(i + 2)
-            if i < NU - 1:
-                q_gy(i)
-            a_gx_tt(i + 2)
-            q_gx(i - 1)
-            if i == NU:
-                q_gy(i - 1)
-            matmuls(i - 1)
-            evacuate(i - 2)
+                rsqrt_on_scalar(rest)
+            if i + 1 != LAST:
+                stage(exp_gy, i + 1)
+            stage(exp_gx, i)
+            if i == LAST:
+                exp_gy(LAST)
+
+            stage(scaled_dy, i + 2)
+            stage(regroup_gx, i - 1)
+            stage(square_dy, i + 2)
+            if i != LAST:
+                stage(quantise_gy, i)
+            stage(squares_on_vector, i + 2)
+            stage(quantise_gx, i - 1)
+            if i - 1 == LAST:
+                quantise_gy(LAST)
+            stage(matmuls, i - 1)
+            stage(store, i - 2)

from contextlib import ExitStack

import concourse.mybir as mybir
from concourse.masks import make_identity

F32 = mybir.dt.float32
BF16 = mybir.dt.bfloat16
I32 = mybir.dt.int32
U32 = mybir.dt.uint32
U8 = mybir.dt.uint8
FP8X4 = mybir.dt.float8_e4m3fn_x4
ACT = mybir.ActivationFunctionType
ALU = mybir.AluOpType

P = 128
PACK = 4
IMAGES = 8
CELLS = 2048
HEIGHT = 256
WIDTH = 512
PASSES = CELLS // (P * PACK)
UNITS = IMAGES * PASSES
LAST = UNITS - 1
COLS = UNITS * PACK
FIRST = PASSES * PACK
MIN_CONFIDENCE = 0.1
MASKED = 1.0e5
LN2 = 0.6931471805599453
SQRT2 = 1.4142135623730951

HEAD_UNITS = 5
TAIL_UNITS = 2

FLOPS = 2 * IMAGES * HEIGHT * WIDTH * CELLS


def vector_cells(k):
    if k < HEAD_UNITS or k >= UNITS - TAIL_UNITS:
        return ()
    return (3,)


def tile_decodepiflayer_kernel(tc, mean, variance, confidence, out):
    nc = tc.nc
    v = nc.vector
    with ExitStack() as ctx:
        consts = ctx.enter_context(tc.tile_pool(name="consts", bufs=1))
        upool = ctx.enter_context(tc.tile_pool(name="upool", bufs=2))
        vpool = ctx.enter_context(tc.tile_pool(name="vpool", bufs=3))
        sqpool = ctx.enter_context(tc.tile_pool(name="sqpool", bufs=4))
        dpool = ctx.enter_context(tc.tile_pool(name="dpool", bufs=3))
        epool = ctx.enter_context(tc.tile_pool(name="epool", bufs=3))
        gpool = ctx.enter_context(tc.tile_pool(name="gpool", bufs=3))
        cpool = ctx.enter_context(tc.tile_pool(name="cpool", bufs=3))
        rpool = ctx.enter_context(tc.tile_pool(name="rpool", bufs=2))
        psum = ctx.enter_context(tc.psum_pool(name="psum", bufs=2))
        xpsum = ctx.enter_context(tc.psum_pool(name="xpsum", bufs=1))
        ctx.enter_context(tc.manual_schedule())

        vb = consts.tile([P, COLS], BF16)
        cb = consts.tile([P, COLS], BF16)
        mb = consts.tile([P, COLS, 2], BF16)
        var_v = variance.rearrange("b h w -> b (h w)").rearrange(
            "b (c p t) -> p b c t", c=PASSES, p=P
        )
        conf_v = confidence.rearrange("b h w -> b (h w)").rearrange(
            "b (c p t) -> p b c t", c=PASSES, p=P
        )
        mean_v = mean.rearrange("b h w x -> b (h w x)").rearrange(
            "b (c p k) -> p b c k", c=PASSES, p=P
        )
        for b0, b1 in ((0, 1), (1, IMAGES)):
            cols = slice(b0 * FIRST, b1 * FIRST)
            nc.sync.dma_start(
                out=vb[:, cols].rearrange("p (b c t) -> p b c t", b=b1 - b0, c=PASSES),
                in_=var_v[:, b0:b1],
            )
            nc.sync.dma_start(
                out=mb[:, cols, :].rearrange("p (b c t) x -> p b c (t x)", b=b1 - b0, c=PASSES),
                in_=mean_v[:, b0:b1],
            )
            nc.sync.dma_start(
                out=cb[:, cols].rearrange("p (b c t) -> p b c t", b=b1 - b0, c=PASSES),
                in_=conf_v[:, b0:b1],
            )

        xi = consts.tile([P, WIDTH], I32)
        xf = consts.tile([P, WIDTH], F32)
        nc.gpsimd.iota(xi[:], pattern=[[1, WIDTH]], base=0, channel_multiplier=0)
        v.tensor_copy(out=xf[:], in_=xi[:])
        ident = consts.tile([P, P], F32)
        make_identity(nc, ident[:])
        xps = xpsum.tile([P, WIDTH], F32)
        nc.tensor.matmul(out=xps[:], lhsT=ident[:], rhs=xf[:], start=True, stop=True)

        def column_tile(name, dtype=F32):
            return consts.tile([P, COLS], dtype, name=name)

        nm = consts.tile([P, 2, COLS], F32)
        v2n = column_tile("v2n")
        ni = column_tile("ni")
        s0 = column_tile("s0")
        s1 = column_tile("s1")
        sv = column_tile("sv")
        ta = column_tile("ta")
        th = column_tile("th")
        cf = column_tile("cf")
        mi = column_tile("mi", I32)
        ei = column_tile("ei", I32)
        ef = column_tile("ef")
        kk = column_tile("kk")
        t1 = column_tile("t1")
        mp = column_tile("mp")
        ek = column_tile("ek")
        e2 = column_tile("e2")
        den = column_tile("den")
        rd = column_tile("rd")
        zz = column_tile("zz")
        ww = column_tile("ww")
        pa = column_tile("pa")
        pb = column_tile("pb")
        msk = column_tile("msk")
        pen = column_tile("pen")
        ll = column_tile("ll")
        lb = column_tile("lb")

        def ts(dst, src, a, b, op0, op1=None):
            if op1 is None:
                return lambda: v.tensor_scalar(out=dst, in0=src, scalar1=a, scalar2=None, op0=op0)
            return lambda: v.tensor_scalar(out=dst, in0=src, scalar1=a, scalar2=b, op0=op0, op1=op1)

        def tt(dst, a, b, op):
            return lambda: v.tensor_tensor(out=dst, in0=a, in1=b, op=op)

        def stt(dst, a, scalar, b, op0, op1):
            return lambda: v.scalar_tensor_tensor(
                out=dst, in0=a, scalar=scalar, in1=b, op0=op0, op1=op1
            )

        def mean_ops(cols):
            return [ts(nm[:, :, cols], mb[:, cols, :].rearrange("p q x -> p x q"), -1.0, None, ALU.mult)]

        def variance_ops(cols):
            return [
                ts(v2n[:, cols], vb[:, cols], -2.0, None, ALU.mult),
                lambda: v.reciprocal(out=ni[:, cols], in_=v2n[:, cols]),
            ]

        def rsqrt_on_scalar(cols):
            nc.scalar.activation(
                out=s0[:, cols], in_=vb[:, cols], func=ACT.Abs_reciprocal_sqrt, scale=2.0
            )

        def newton_ops(cols):
            ops = []
            for src, dst in ((s0, s1), (s1, sv)):
                ops.append(stt(ta[:, cols], src[:, cols], 0.5, src[:, cols], ALU.mult, ALU.mult))
                ops.append(tt(th[:, cols], ta[:, cols], v2n[:, cols], ALU.mult))
                ops.append(stt(dst[:, cols], th[:, cols], 1.5, src[:, cols], ALU.add, ALU.mult))
            return ops

        def confidence_ops(cols):
            bits = cf[:, cols].bitcast(I32)
            m = mi[:, cols].bitcast(F32)
            return [
                lambda: v.tensor_copy(out=cf[:, cols], in_=cb[:, cols]),
                ts(mi[:, cols], bits, 0x007FFFFF, 0x3F800000, ALU.bitwise_and, ALU.bitwise_or),
                ts(ei[:, cols], bits, 23, None, ALU.arith_shift_right),
                ts(kk[:, cols], m, SQRT2, None, ALU.is_gt),
                lambda: v.tensor_copy(out=ef[:, cols], in_=ei[:, cols]),
                ts(t1[:, cols], kk[:, cols], -0.5, 1.0, ALU.mult, ALU.add),
                tt(ek[:, cols], ef[:, cols], kk[:, cols], ALU.add),
                tt(mp[:, cols], m, t1[:, cols], ALU.mult),
                ts(e2[:, cols], ek[:, cols], -127.0, LN2, ALU.add, ALU.mult),
                ts(den[:, cols], mp[:, cols], 1.0, None, ALU.add),
                ts(msk[:, cols], cf[:, cols], MIN_CONFIDENCE, None, ALU.is_gt),
                lambda: v.reciprocal(out=rd[:, cols], in_=den[:, cols]),
                ts(pen[:, cols], msk[:, cols], -1.0, MASKED, ALU.add, ALU.mult),
                stt(zz[:, cols], mp[:, cols], -1.0, rd[:, cols], ALU.add, ALU.mult),
                tt(ww[:, cols], zz[:, cols], zz[:, cols], ALU.mult),
                ts(pa[:, cols], ww[:, cols], 1.0 / 11.0, None, ALU.mult),
                stt(pb[:, cols], pa[:, cols], 1.0 / 9.0, ww[:, cols], ALU.add, ALU.mult),
                stt(pa[:, cols], pb[:, cols], 1.0 / 7.0, ww[:, cols], ALU.add, ALU.mult),
                stt(pb[:, cols], pa[:, cols], 1.0 / 5.0, ww[:, cols], ALU.add, ALU.mult),
                stt(pa[:, cols], pb[:, cols], 1.0 / 3.0, ww[:, cols], ALU.add, ALU.mult),
                stt(pb[:, cols], pa[:, cols], 1.0, zz[:, cols], ALU.add, ALU.mult),
                stt(ll[:, cols], pb[:, cols], 2.0, e2[:, cols], ALU.mult, ALU.add),
                tt(lb[:, cols], ll[:, cols], pen[:, cols], ALU.add),
            ]

        first = slice(0, FIRST)
        rest = slice(FIRST, COLS)
        queues = {"first": confidence_ops(first), "rest": []}
        issued = {"first": 0, "rest": 0}

        def issue(name):
            if issued[name] < len(queues[name]):
                queues[name][issued[name]]()
                issued[name] = issued[name] + 1

        def fill():
            issue("first")
            issue("rest")

        for op in mean_ops(first) + variance_ops(first):
            op()
        rsqrt_on_scalar(first)
        issue("first")
        issue("first")
        for op in newton_ops(first):
            op()
            issue("first")

        tiles = {}

        def col(tile, k, t):
            return tile[:, k * PACK + t : k * PACK + t + 1]

        def scaled_dy(k):
            u = upool.tile([P, PACK, HEIGHT], F32)
            tiles["u", k] = u
            for t in range(PACK):
                v.tensor_scalar(
                    out=u[:, t, :], in0=xf[:, 0:HEIGHT], scalar1=col(nm[:, 1, :], k, t),
                    scalar2=col(sv, k, t), op0=ALU.add, op1=ALU.mult,
                )
                fill()

        def square_dy(k):
            v2 = vpool.tile([P, HEIGHT, PACK], F32)
            tiles["v2", k] = v2
            pairs = tiles["u", k][:].rearrange("p t (c i) -> p c t i", i=2)
            v.tensor_tensor(
                out=v2[:].rearrange("p (c i) t -> p c t i", i=2), in0=pairs, in1=pairs, op=ALU.mult
            )
            fill()

        def exp_gy(k):
            pieces = 2 if k == LAST else 1
            gy = gpool.tile([P, HEIGHT * PACK], BF16, align_bytes=64)
            tiles["gy", k] = gy
            flat = tiles["v2", k][:].rearrange("p w t -> p (w t)")
            width = HEIGHT * PACK // pieces
            for h in range(pieces):
                part = slice(h * width, (h + 1) * width)
                nc.scalar.activation(out=gy[:, part], in_=flat[:, part], func=ACT.Exp, scale=-1.0)

        def quantise_gy(k):
            pieces = 2 if k == LAST else 1
            gyc = cpool.tile([P, HEIGHT], U32, align_bytes=64)
            gys = cpool.tile([P, HEIGHT], U8, align_bytes=64)
            tiles["gyc", k] = gyc
            tiles["gys", k] = gys
            width = HEIGHT // pieces
            for h in range(pieces):
                part = slice(h * width, (h + 1) * width)
                v.quantize_mx(
                    out=gyc[:, part].bitcast(FP8X4), scales=gys[:, part],
                    in_=tiles["gy", k][:, h * width * PACK : (h + 1) * width * PACK],
                )
                fill()

        def squares_tile(k):
            if ("sq", k) not in tiles:
                sq = sqpool.tile([P, PACK, WIDTH], F32)
                tiles["sq", k] = sq
            return tiles["sq", k]

        def dx_on_gpsimd(k):
            for t in vector_cells(k):
                d = dpool.tile([P, WIDTH], F32)
                tiles["d", k, t] = d
                nc.gpsimd.tensor_scalar(
                    out=d[:], in0=xf[:], scalar1=col(nm[:, 0, :], k, t), scalar2=1.0,
                    op0=ALU.add, op1=ALU.mult,
                )

        def squares_on_vector(k):
            sq = squares_tile(k)
            for t in vector_cells(k):
                v.scalar_tensor_tensor(
                    out=sq[:, t, :], in0=xps[:], scalar=col(nm[:, 0, :], k, t),
                    in1=tiles["d", k, t][:], op0=ALU.add, op1=ALU.mult,
                )
                fill()

        def squares_on_scalar(k):
            sq = squares_tile(k)
            for t in range(PACK):
                if t not in vector_cells(k):
                    nc.scalar.activation(
                        out=sq[:, t, :], in_=xf[:], func=ACT.Square,
                        bias=mb[:, k * PACK + t, 0:1], scale=-1.0,
                    )

        def exp_gx(k):
            e = epool.tile([P, PACK, WIDTH], BF16)
            tiles["e", k] = e
            for t in range(PACK):
                nc.scalar.activation(
                    out=e[:, t, :], in_=tiles["sq", k][:, t, :], func=ACT.Exp,
                    bias=col(lb, k, t), scale=col(ni, k, t),
                )

        def regroup_gx(k):
            gx = gpool.tile([P, WIDTH, PACK], BF16, align_bytes=64)
            tiles["gx", k] = gx
            v.tensor_copy(
                out=gx[:].rearrange("p (c i) t -> p c t i", i=4),
                in_=tiles["e", k][:].rearrange("p t (c i) -> p c t i", i=4),
            )
            fill()

        def quantise_gx(k):
            gxc = cpool.tile([P, WIDTH], U32, align_bytes=64)
            gxs = cpool.tile([P, WIDTH], U8, align_bytes=64)
            tiles["gxc", k] = gxc
            tiles["gxs", k] = gxs
            v.quantize_mx(
                out=gxc[:].bitcast(FP8X4), scales=gxs[:],
                in_=tiles["gx", k][:].rearrange("p w t -> p (w t)"),
            )
            fill()

        def matmuls(k):
            b, c = divmod(k, PASSES)
            if c == 0:
                acc0 = psum.tile([P, WIDTH], F32)
                acc1 = psum.tile([P, WIDTH], F32)
                tiles["acc", b, 0] = acc0
                tiles["acc", b, 1] = acc1
            for m in range(HEIGHT // P):
                rows = slice(m * P, (m + 1) * P)
                nc.tensor.matmul_mx(
                    out=tiles["acc", b, m][:],
                    lhsT=tiles["gyc", k][:, rows].bitcast(FP8X4),
                    lhsT_scale=tiles["gys", k][:, rows],
                    rhs=tiles["gxc", k][:].bitcast(FP8X4),
                    rhs_scale=tiles["gxs", k][:],
                    start=(c == 0),
                    stop=(c == PASSES - 1),
                )

        def store(k):
            b, c = divmod(k, PASSES)
            if c != PASSES - 1:
                return
            res0 = rpool.tile([P, WIDTH], F32)
            res1 = rpool.tile([P, WIDTH], F32)
            v.tensor_copy(out=res0[:], in_=tiles["acc", b, 0][:])
            if k == LAST:
                nc.scalar.copy(out=res1[:], in_=tiles["acc", b, 1][:])
            else:
                v.tensor_copy(out=res1[:], in_=tiles["acc", b, 1][:])
            nc.sync.dma_start(out=out[b, 0:P, :], in_=res0[:])
            nc.sync.dma_start(out=out[b, P : 2 * P, :], in_=res1[:])

        def stage(fn, k):
            if 0 <= k < UNITS:
                fn(k)

        needed_first = variance_ops(rest) + newton_ops(rest) + mean_ops(rest)
        stage(dx_on_gpsimd, 0)
        for i in range(-2, UNITS + 2):
            if i == -1:
                queues["rest"].extend(needed_first + confidence_ops(rest))
            if i == 0:
                while issued["first"] < len(queues["first"]):
                    issue("first")
            if i == PASSES - 2:
                assert issued["rest"] >= len(needed_first)
            if i == PASSES:
                assert issued["rest"] == len(queues["rest"])

            stage(dx_on_gpsimd, i + 3)

            stage(squares_on_scalar, i + 2)
            if i == -1:
                rsqrt_on_scalar(rest)
            if i + 1 != LAST:
                stage(exp_gy, i + 1)
            stage(exp_gx, i)
            if i == LAST:
                exp_gy(LAST)

            stage(scaled_dy, i + 2)
            stage(regroup_gx, i - 1)
            stage(square_dy, i + 2)
            if i != LAST:
                stage(quantise_gy, i)
            stage(squares_on_vector, i + 2)
            stage(quantise_gx, i - 1)
            if i - 1 == LAST:
                quantise_gy(LAST)
            stage(matmuls, i - 1)
            stage(store, i - 2)
